import numpy as np
import ml_dtypes


def mxq(x, axis, fmt="e4m3"):
    dtype, down = {"e4m3": (ml_dtypes.float8_e4m3fn, 7), "e5m2": (ml_dtypes.float8_e5m2, 14)}[fmt]
    v = np.moveaxis(np.asarray(x, np.float32).astype(ml_dtypes.bfloat16).astype(np.float64), axis, -1)
    blocks = v.reshape(v.shape[:-1] + (-1, 32))
    amax = np.abs(blocks).max(-1, keepdims=True)
    byte = np.maximum(np.where(amax > 0, np.frexp(amax)[1] - 1 + 127, 0) - down, 1)
    scale = np.exp2(byte - 127.0)
    codes = (blocks / scale).astype(np.float32).astype(dtype).astype(np.float64)
    return np.moveaxis((codes * scale).reshape(v.shape), -1, axis)


WIDE = False


def mx_kscale(k):
    if not WIDE:
        return np.ones(k)
    levels = np.array([10, -10, 5, -5, 0])
    a = np.random.permutation(np.resize(levels, k // 512 * 4)).reshape(k // 512, 4)
    idx = np.arange(k)
    return np.exp2(a[idx // 512, idx % 128 // 32])


BF16 = ml_dtypes.bfloat16


def bf(x):
    return np.asarray(x, np.float32).astype(BF16)


def f64(x):
    return np.asarray(x).astype(np.float64)


E2M1 = np.array([0.0, 0.5, 1.0, 1.5, 2.0, 3.0, 4.0, 6.0, -0.0, -0.5, -1.0, -1.5, -2.0, -3.0, -4.0, -6.0])


def pack_weight(w, fmt):
    k, n = w.shape
    w = f64(bf(w)).reshape(k // 32, 32, n)
    amax = np.abs(w).max(1)
    if fmt == "e4m3":
        byte = np.frexp(amax)[1] - 1 + 127 - 7
    else:
        mant, ex = np.frexp(amax / 6.0)
        byte = np.where(mant > 0.5, ex, ex - 1) + 127
    byte = np.clip(np.where(amax > 0, byte, 1), 1, 254)
    scaled = (w * np.exp2(127.0 - byte)[:, None, :]).reshape(k, n).astype(np.float32)
    by_word = np.ascontiguousarray(scaled.reshape(k // 512, 128, 4, n).transpose(0, 1, 3, 2))
    if fmt == "e4m3":
        words = by_word.astype(ml_dtypes.float8_e4m3fn).view(np.uint8)
    else:
        c = by_word.astype(ml_dtypes.float4_e2m1fn).view(np.uint8) & 0xF
        words = c[..., 0::2] | (c[..., 1::2] << 4)
    return np.ascontiguousarray(words), np.ascontiguousarray(byte.astype(np.uint8).reshape(k // 512, 16, n))


def unpack_weight(words, scales, fmt):
    g, p, n, _ = words.shape
    if fmt == "e4m3":
        vals = np.ascontiguousarray(words).view(ml_dtypes.float8_e4m3fn).astype(np.float64)
    else:
        nib = np.empty((g, p, n, 4), np.uint8)
        nib[..., 0::2] = words & 0xF
        nib[..., 1::2] = words >> 4
        vals = E2M1[nib]
    vals = vals * np.repeat(np.exp2(scales.astype(np.float64) - 127.0), 8, axis=1)[..., None]
    return vals.transpose(0, 1, 3, 2).reshape(g * 512, n)

def pack4(w):
    words, scales = pack_weight(w, "e2m1")
    return words.reshape(words.shape[0], 128, -1), scales


def unpack4(words, scales):
    return unpack_weight(words.reshape(words.shape[0], 128, -1, 2), scales, "e2m1")


B, S, DIM, H, NOPE, ROPE_D, VD = 2, 128, 2048, 16, 128, 64, 128
QKD = NOPE + ROPE_D
BASE = 10000.0


def rope_cos_sin(seq_len):
    theta = 1.0 / BASE ** (f64(np.arange(0, ROPE_D, 2)) / ROPE_D)
    pos = f64(np.arange(seq_len))
    ang = pos[:, None] * theta[None, :]
    return np.cos(ang), np.sin(ang)


def apply_rope(v, cos, sin):
    b, s, h, d = v.shape
    vs = v.reshape(b, s, h, d // 2, 2)
    c = cos[None, :, None, :]
    sn = sin[None, :, None, :]
    out = np.stack([vs[..., 0] * c - vs[..., 1] * sn, vs[..., 1] * c + vs[..., 0] * sn], axis=-1)
    return out.reshape(b, s, h, d)


def setup_inputs():
    s = mx_kscale(DIM)
    x = bf(np.random.standard_normal((B, S, DIM)) * s)
    Wq_words, Wq_scales = pack4(np.random.standard_normal((DIM, H * QKD)) / np.sqrt(DIM) / s[:, None])
    Wk_words, Wk_scales = pack4(np.random.standard_normal((DIM, H * QKD)) / np.sqrt(DIM) / s[:, None])
    return {'x': x,
            'Wq_words': Wq_words, 'Wq_scales': Wq_scales,
            'Wk_words': Wk_words, 'Wk_scales': Wk_scales}


def reference(x, Wq_words, Wq_scales, Wk_words, Wk_scales):
    xq = mxq(f64(x), 2, 'e4m3')
    q = (xq @ unpack4(Wq_words, Wq_scales)).reshape(B, S, H, QKD)
    k = (xq @ unpack4(Wk_words, Wk_scales)).reshape(B, S, H, QKD)
    cos, sin = rope_cos_sin(S)
    q = np.concatenate([q[..., :NOPE], apply_rope(q[..., NOPE:], cos, sin)], axis=-1)
    k = np.concatenate([k[..., :NOPE], apply_rope(k[..., NOPE:], cos, sin)], axis=-1)
    return q, k

@@ -1,0 +1,187 @@
+import math
+from contextlib import ExitStack
+
+import concourse.mybir as mybir
+from concourse.masks import make_identity
+
+F32 = mybir.dt.float32
+BF16 = mybir.dt.bfloat16
+I32 = mybir.dt.int32
+U32 = mybir.dt.uint32
+U8 = mybir.dt.uint8
+FP8X4 = mybir.dt.float8_e4m3fn_x4
+FP4X4 = mybir.dt.float4_e2m1fn_x4
+ALU = mybir.AluOpType
+ACT = mybir.ActivationFunctionType
+
+P = 128
+SEQS = 2
+DIM = 2048
+HEADS = 16
+NOPE = 128
+ROPE = 64
+HEAD = NOPE + ROPE
+PAIRS = ROPE // 2
+BASE = 10000.0
+
+PACK = 4
+K_PASS = P * PACK
+PASSES = DIM // K_PASS
+BANK = 512
+STAGE_HEADS = 8
+STAGE_COLS = STAGE_HEADS * HEAD
+STAGE_BANKS = STAGE_COLS // BANK
+STAGES = HEADS // STAGE_HEADS
+SCALE_ROWS = K_PASS // 32
+
+FLOPS = 2 * SEQS * P * DIM * 2 * HEADS * HEAD
+
+
+def load_scale_rows(nc, plane, scales, cols):
+    by_row = scales.rearrange("g q n -> q g n")
+    for q in range(SCALE_ROWS // 2):
+        first = 32 * (q // 4) + q % 4
+        nc.sync.dma_start(
+            out=plane[first:P:64, :, :].bitcast(I32),
+            in_=by_row[q : SCALE_ROWS : SCALE_ROWS // 2, :, cols].bitcast(I32),
+        )
+
+
+def build_rotation_tables(nc, keep):
+    position = keep.tile([P, 1], I32)
+    nc.gpsimd.iota(position[:], pattern=[[0, 1]], base=0, channel_multiplier=1)
+    angle = keep.tile([P, PAIRS], F32)
+    nc.vector.tensor_copy(out=angle[:, 0:1], in_=position[:])
+    for width in (1, 2, 4, 8, 16):
+        nc.vector.tensor_scalar_mul(
+            angle[:, width : 2 * width], angle[:, 0:width], BASE ** (-2.0 * width / ROPE)
+        )
+    turns = keep.tile([P, 2, PAIRS], F32)
+    nc.vector.tensor_scalar(
+        out=turns[:, 0, :], in0=angle[:], scalar1=0.5 / math.pi, scalar2=0.25,
+        op0=ALU.mult, op1=ALU.add,
+    )
+    nc.vector.tensor_scalar_mul(turns[:, 1, :], angle[:], 0.5 / math.pi)
+    whole_int = keep.tile([P, 2, PAIRS], I32)
+    nc.vector.tensor_copy(out=whole_int[:], in_=turns[:])
+    whole = keep.tile([P, 2, PAIRS], F32)
+    nc.vector.tensor_copy(out=whole[:], in_=whole_int[:])
+    nc.vector.tensor_sub(turns[:], turns[:], whole[:])
+    nc.vector.tensor_single_scalar(out=whole[:], in_=turns[:], scalar=0.5, op=ALU.is_gt)
+    nc.vector.tensor_sub(turns[:], turns[:], whole[:])
+
+    cos_twice = keep.tile([P, PAIRS, 2], F32)
+    sin_minus = keep.tile([P, PAIRS], F32)
+    sin_plus = keep.tile([P, PAIRS], F32)
+    nc.scalar.activation(
+        out=cos_twice[:], in_=turns[:, 0, :].unsqueeze(2).to_broadcast([P, PAIRS, 2]),
+        func=ACT.Sin, scale=2.0 * math.pi,
+    )
+    nc.scalar.activation(out=sin_minus[:], in_=turns[:, 1, :], func=ACT.Sin, scale=-2.0 * math.pi)
+    nc.scalar.activation(out=sin_plus[:], in_=turns[:, 1, :], func=ACT.Sin, scale=2.0 * math.pi)
+    return cos_twice, sin_minus, sin_plus
+
+
+def rotate(nc, work, rope, tables):
+    cos_twice, sin_minus, sin_plus = tables
+    heads = rope.shape[1]
+    pairs = rope.rearrange("p h (i two) -> p h i two", two=2)
+    straight = work.tile([P, heads, PAIRS, 2], F32, tag="straight")
+    nc.vector.tensor_mul(
+        straight[:], pairs, cos_twice[:].unsqueeze(1).to_broadcast([P, heads, PAIRS, 2])
+    )
+    crossed = work.tile([P, heads, 2, PAIRS], F32, tag="crossed")
+    nc.vector.tensor_mul(
+        crossed[:, :, 0, :], pairs[:, :, :, 1],
+        sin_minus[:].unsqueeze(1).to_broadcast([P, heads, PAIRS]),
+    )
+    nc.vector.tensor_mul(
+        crossed[:, :, 1, :], pairs[:, :, :, 0],
+        sin_plus[:].unsqueeze(1).to_broadcast([P, heads, PAIRS]),
+    )
+    nc.vector.tensor_add(pairs, straight[:], crossed[:].rearrange("p h two i -> p h i two"))
+
+
+def tile_mla_pa_kernel(tc, x, Wq_words, Wq_scales, Wk_words, Wk_scales, out_0, out_1):
+    nc = tc.nc
+    weights = ((Wq_words, Wq_scales, out_0), (Wk_words, Wk_scales, out_1))
+    with ExitStack() as ctx:
+        keep = ctx.enter_context(tc.tile_pool(name="keep", bufs=1))
+        work = ctx.enter_context(tc.tile_pool(name="work", bufs=3))
+        psum = ctx.enter_context(tc.psum_pool(name="psum", bufs=8))
+
+        x_sb = keep.tile([P, SEQS, DIM], BF16)
+        for b in range(SEQS):
+            nc.sync.dma_start(out=x_sb[:, b, :], in_=x[b])
+
+        stages = []
+        for words_in, scales_in, out in weights:
+            for half in range(STAGES):
+                n = len(stages)
+                col0 = half * STAGE_COLS
+                plane = keep.tile([P, PASSES, STAGE_COLS], U8, name="plane%d" % n, align_bytes=64)
+                nc.vector.memset(plane[:].bitcast(I32), 0)
+                load_scale_rows(nc, plane, scales_in, slice(col0, col0 + STAGE_COLS))
+                words = keep.tile([P, PASSES, 2 * STAGE_COLS], U8, name="words%d" % n, align_bytes=64)
+                by_partition = words_in.rearrange("g p n -> p g n")
+                pieces = STAGE_BANKS if n == 0 else 1
+                width = 2 * STAGE_COLS // pieces
+                for piece in range(pieces):
+                    lo = piece * width
+                    nc.sync.dma_start(
+                        out=words[:, :, lo : lo + width].bitcast(I32),
+                        in_=by_partition[:, :, 2 * col0 + lo : 2 * col0 + lo + width].bitcast(I32),
+                    )
+                stages.append((plane, words, out, half))
+
+        tables = build_rotation_tables(nc, keep)
+
+        ident = keep.tile([P, P], F32)
+        make_identity(nc, ident[:])
+        grouped = keep.tile([P, SEQS, PASSES, P, PACK], BF16, align_bytes=64)
+        x_codes = keep.tile([P, SEQS, PASSES, P], U32, align_bytes=64)
+        x_scales = keep.tile([P, SEQS, PASSES, P], U8, align_bytes=64)
+        for b in range(SEQS):
+            x_words = x_sb[:, b, :].bitcast(F32)
+            for pair in range(PASSES // 2):
+                bank = psum.tile([P, BANK], F32, tag="bank")
+                for slot in range(4):
+                    g, u = 2 * pair + slot // 2, slot % 2
+                    nc.tensor.transpose(
+                        bank[:, slot * P : (slot + 1) * P],
+                        x_words[:, 256 * g + u : 256 * (g + 1) : 2],
+                        ident[:],
+                    )
+                copy = nc.vector.tensor_copy if pair % 2 == 0 else nc.scalar.copy
+                copy(
+                    out=grouped[:, b, 2 * pair : 2 * pair + 2, :, :].bitcast(F32),
+                    in_=bank[:].rearrange("p (g u m) -> p g m u", g=2, u=2),
+                )
+            nc.vector.quantize_mx(
+                out=x_codes[:, b].rearrange("p g m -> p (g m)").bitcast(FP8X4),
+                scales=x_scales[:, b].rearrange("p g m -> p (g m)"),
+                in_=grouped[:, b].rearrange("p g m t -> p (g m t)"),
+            )
+
+        for n, (plane, words, out, half) in enumerate(stages):
+            for b in range(SEQS):
+                result = keep.tile([P, STAGE_HEADS, HEAD], F32, name="result%d_%d" % (n, b))
+                flat = result[:].rearrange("p h d -> p (h d)")
+                for j in range(STAGE_BANKS):
+                    acc = psum.tile([P, BANK], F32, tag="bank")
+                    for g in range(PASSES):
+                        nc.tensor.matmul_mx(
+                            out=acc[:],
+                            lhsT=x_codes[:, b, g, :].bitcast(FP8X4),
+                            lhsT_scale=x_scales[:, b, g, :],
+                            rhs=words[:, g, 2 * j * BANK : 2 * (j + 1) * BANK].bitcast(FP4X4),
+                            rhs_scale=plane[:, g, j * BANK : (j + 1) * BANK],
+                            start=(g == 0),
+                            stop=(g == PASSES - 1),
+                        )
+                    nc.scalar.copy(out=flat[:, j * BANK : (j + 1) * BANK], in_=acc[:])
+                    mine = [h for h in range(STAGE_HEADS) if (h * HEAD + NOPE) // BANK == j]
+                    rotate(nc, work, result[:, mine[0] : mine[-1] + 1, NOPE:HEAD], tables)
+                nc.sync.dma_start(
+                    out=out[b, :, half * STAGE_HEADS : (half + 1) * STAGE_HEADS, :], in_=result[:]
+                )

@@ -39,11 +39,10 @@ FLOPS = 2 * SEQS * P * DIM * 2 * HEADS * HEAD
 
 def load_scale_rows(nc, plane, scales, cols):
     by_row = scales.rearrange("g q n -> q g n")
-    for q in range(SCALE_ROWS // 2):
-        first = 32 * (q // 4) + q % 4
+    for r in range(4):
         nc.sync.dma_start(
-            out=plane[first:P:64, :, :].bitcast(I32),
-            in_=by_row[q : SCALE_ROWS : SCALE_ROWS // 2, :, cols].bitcast(I32),
+            out=plane[r:P:32, :, :].bitcast(I32),
+            in_=by_row[r:SCALE_ROWS:4, :, cols].bitcast(I32),
         )
 
 
@@ -104,37 +103,36 @@ def rotate(nc, work, rope, tables):
 
 def tile_mla_pa_kernel(tc, x, Wq_words, Wq_scales, Wk_words, Wk_scales, out_0, out_1):
     nc = tc.nc
-    weights = ((Wq_words, Wq_scales, out_0), (Wk_words, Wk_scales, out_1))
     with ExitStack() as ctx:
         keep = ctx.enter_context(tc.tile_pool(name="keep", bufs=1))
         work = ctx.enter_context(tc.tile_pool(name="work", bufs=3))
         psum = ctx.enter_context(tc.psum_pool(name="psum", bufs=8))
+        ctx.enter_context(tc.manual_schedule())
 
         x_sb = keep.tile([P, SEQS, DIM], BF16)
         for b in range(SEQS):
             nc.sync.dma_start(out=x_sb[:, b, :], in_=x[b])
 
-        stages = []
-        for words_in, scales_in, out in weights:
-            for half in range(STAGES):
-                n = len(stages)
-                col0 = half * STAGE_COLS
-                plane = keep.tile([P, PASSES, STAGE_COLS], U8, name="plane%d" % n, align_bytes=64)
-                nc.vector.memset(plane[:].bitcast(I32), 0)
-                load_scale_rows(nc, plane, scales_in, slice(col0, col0 + STAGE_COLS))
-                words = keep.tile([P, PASSES, 2 * STAGE_COLS], U8, name="words%d" % n, align_bytes=64)
-                by_partition = words_in.rearrange("g p n -> p g n")
-                pieces = STAGE_BANKS if n == 0 else 1
-                width = 2 * STAGE_COLS // pieces
-                for piece in range(pieces):
-                    lo = piece * width
-                    nc.sync.dma_start(
-                        out=words[:, :, lo : lo + width].bitcast(I32),
-                        in_=by_partition[:, :, 2 * col0 + lo : 2 * col0 + lo + width].bitcast(I32),
-                    )
-                stages.append((plane, words, out, half))
+        def load_stage(words_in, scales_in, col0, pieces):
+            plane = keep.tile([P, PASSES, STAGE_COLS], U8, name="plane%d" % len(stages), align_bytes=64)
+            nc.vector.memset(plane[:].bitcast(I32), 0)
+            load_scale_rows(nc, plane, scales_in, slice(col0, col0 + STAGE_COLS))
+            words = keep.tile([P, PASSES, 2 * STAGE_COLS], U8, name="words%d" % len(stages), align_bytes=64)
+            by_partition = words_in.rearrange("g p n -> p g n")
+            width = 2 * STAGE_COLS // pieces
+            for lo in range(0, 2 * STAGE_COLS, width):
+                nc.sync.dma_start(
+                    out=words[:, :, lo : lo + width].bitcast(I32),
+                    in_=by_partition[:, :, 2 * col0 + lo : 2 * col0 + lo + width].bitcast(I32),
+                )
+            stages.append((plane, words))
 
+        stages = []
+        load_stage(Wq_words, Wq_scales, 0, STAGE_BANKS)
         tables = build_rotation_tables(nc, keep)
+        load_stage(Wq_words, Wq_scales, STAGE_COLS, 1)
+        load_stage(Wk_words, Wk_scales, 0, 1)
+        load_stage(Wk_words, Wk_scales, STAGE_COLS, 1)
 
         ident = keep.tile([P, P], F32)
         make_identity(nc, ident[:])
@@ -152,8 +150,7 @@ def tile_mla_pa_kernel(tc, x, Wq_words, Wq_scales, Wk_words, Wk_scales, out_0, o
                         x_words[:, 256 * g + u : 256 * (g + 1) : 2],
                         ident[:],
                     )
-                copy = nc.vector.tensor_copy if pair % 2 == 0 else nc.scalar.copy
-                copy(
+                nc.scalar.copy(
                     out=grouped[:, b, 2 * pair : 2 * pair + 2, :, :].bitcast(F32),
                     in_=bank[:].rearrange("p (g u m) -> p g m u", g=2, u=2),
                 )
@@ -163,11 +160,17 @@ def tile_mla_pa_kernel(tc, x, Wq_words, Wq_scales, Wk_words, Wk_scales, out_0, o
                 in_=grouped[:, b].rearrange("p g m t -> p (g m t)"),
             )
 
-        for n, (plane, words, out, half) in enumerate(stages):
+        for n, (plane, words) in enumerate(stages):
+            out, half = (out_0, out_1)[n // STAGES], n % STAGES
             for b in range(SEQS):
                 result = keep.tile([P, STAGE_HEADS, HEAD], F32, name="result%d_%d" % (n, b))
                 flat = result[:].rearrange("p h d -> p (h d)")
+                out_flat = out[b].rearrange("s h d -> s (h d)")[
+                    :, half * STAGE_COLS : (half + 1) * STAGE_COLS
+                ]
+                last = n == len(stages) - 1 and b == SEQS - 1
                 for j in range(STAGE_BANKS):
+                    bank_cols = slice(j * BANK, (j + 1) * BANK)
                     acc = psum.tile([P, BANK], F32, tag="bank")
                     for g in range(PASSES):
                         nc.tensor.matmul_mx(
@@ -175,13 +178,14 @@ def tile_mla_pa_kernel(tc, x, Wq_words, Wq_scales, Wk_words, Wk_scales, out_0, o
                             lhsT=x_codes[:, b, g, :].bitcast(FP8X4),
                             lhsT_scale=x_scales[:, b, g, :],
                             rhs=words[:, g, 2 * j * BANK : 2 * (j + 1) * BANK].bitcast(FP4X4),
-                            rhs_scale=plane[:, g, j * BANK : (j + 1) * BANK],
+                            rhs_scale=plane[:, g, bank_cols],
                             start=(g == 0),
                             stop=(g == PASSES - 1),
                         )
-                    nc.scalar.copy(out=flat[:, j * BANK : (j + 1) * BANK], in_=acc[:])
+                    nc.scalar.copy(out=flat[:, bank_cols], in_=acc[:])
                     mine = [h for h in range(STAGE_HEADS) if (h * HEAD + NOPE) // BANK == j]
                     rotate(nc, work, result[:, mine[0] : mine[-1] + 1, NOPE:HEAD], tables)
-                nc.sync.dma_start(
-                    out=out[b, :, half * STAGE_HEADS : (half + 1) * STAGE_HEADS, :], in_=result[:]
-                )
+                    if last:
+                        nc.sync.dma_start(out=out_flat[:, bank_cols], in_=flat[:, bank_cols])
+                if not last:
+                    nc.sync.dma_start(out=out_flat, in_=flat)

@@ -33,40 +33,35 @@ STAGE_COLS = STAGE_HEADS * HEAD
 STAGE_BANKS = STAGE_COLS // BANK
 STAGES = HEADS // STAGE_HEADS
 SCALE_ROWS = K_PASS // 32
+ROUND = 1.5 * 2.0**23
 
 FLOPS = 2 * SEQS * P * DIM * 2 * HEADS * HEAD
 
 
-def load_scale_rows(nc, plane, scales, cols):
+def load_scale_rows(nc, plane, scales, col0):
     by_row = scales.rearrange("g q n -> q g n")
-    for r in range(4):
+    for q in range(SCALE_ROWS // 2):
+        first = 32 * (q // 4) + q % 4
         nc.sync.dma_start(
-            out=plane[r:P:32, :, :].bitcast(I32),
-            in_=by_row[r:SCALE_ROWS:4, :, cols].bitcast(I32),
+            out=plane[first:P:64, :, :].bitcast(I32),
+            in_=by_row[q : SCALE_ROWS : SCALE_ROWS // 2, :, col0 : col0 + STAGE_COLS].bitcast(I32),
         )
 
 
 def build_rotation_tables(nc, keep):
     position = keep.tile([P, 1], I32)
     nc.gpsimd.iota(position[:], pattern=[[0, 1]], base=0, channel_multiplier=1)
-    angle = keep.tile([P, PAIRS], F32)
-    nc.vector.tensor_copy(out=angle[:, 0:1], in_=position[:])
+    turns = keep.tile([P, 2, PAIRS], F32)
+    nc.vector.tensor_scalar_mul(turns[:, 1, 0:1], position[:], 0.5 / math.pi)
     for width in (1, 2, 4, 8, 16):
         nc.vector.tensor_scalar_mul(
-            angle[:, width : 2 * width], angle[:, 0:width], BASE ** (-2.0 * width / ROPE)
+            turns[:, 1, width : 2 * width], turns[:, 1, 0:width], BASE ** (-2.0 * width / ROPE)
         )
-    turns = keep.tile([P, 2, PAIRS], F32)
-    nc.vector.tensor_scalar(
-        out=turns[:, 0, :], in0=angle[:], scalar1=0.5 / math.pi, scalar2=0.25,
-        op0=ALU.mult, op1=ALU.add,
-    )
-    nc.vector.tensor_scalar_mul(turns[:, 1, :], angle[:], 0.5 / math.pi)
-    whole_int = keep.tile([P, 2, PAIRS], I32)
-    nc.vector.tensor_copy(out=whole_int[:], in_=turns[:])
+    nc.vector.tensor_scalar_add(turns[:, 0, :], turns[:, 1, :], 0.25)
     whole = keep.tile([P, 2, PAIRS], F32)
-    nc.vector.tensor_copy(out=whole[:], in_=whole_int[:])
-    nc.vector.tensor_sub(turns[:], turns[:], whole[:])
-    nc.vector.tensor_single_scalar(out=whole[:], in_=turns[:], scalar=0.5, op=ALU.is_gt)
+    nc.vector.tensor_scalar(
+        out=whole[:], in0=turns[:], scalar1=ROUND, scalar2=ROUND, op0=ALU.add, op1=ALU.subtract
+    )
     nc.vector.tensor_sub(turns[:], turns[:], whole[:])
 
     cos_twice = keep.tile([P, PAIRS, 2], F32)
@@ -109,30 +104,28 @@ def tile_mla_pa_kernel(tc, x, Wq_words, Wq_scales, Wk_words, Wk_scales, out_0, o
         psum = ctx.enter_context(tc.psum_pool(name="psum", bufs=8))
         ctx.enter_context(tc.manual_schedule())
 
+        zero = keep.tile([P, 1], F32)
+        nc.vector.memset(zero[:], 0.0)
+        nc.scalar.activation(out=zero[:], in_=zero[:], func=ACT.Sin)
+
         x_sb = keep.tile([P, SEQS, DIM], BF16)
         for b in range(SEQS):
             nc.sync.dma_start(out=x_sb[:, b, :], in_=x[b])
 
-        def load_stage(words_in, scales_in, col0, pieces):
-            plane = keep.tile([P, PASSES, STAGE_COLS], U8, name="plane%d" % len(stages), align_bytes=64)
-            nc.vector.memset(plane[:].bitcast(I32), 0)
-            load_scale_rows(nc, plane, scales_in, slice(col0, col0 + STAGE_COLS))
-            words = keep.tile([P, PASSES, 2 * STAGE_COLS], U8, name="words%d" % len(stages), align_bytes=64)
-            by_partition = words_in.rearrange("g p n -> p g n")
-            width = 2 * STAGE_COLS // pieces
-            for lo in range(0, 2 * STAGE_COLS, width):
-                nc.sync.dma_start(
-                    out=words[:, :, lo : lo + width].bitcast(I32),
-                    in_=by_partition[:, :, 2 * col0 + lo : 2 * col0 + lo + width].bitcast(I32),
-                )
-            stages.append((plane, words))
-
         stages = []
-        load_stage(Wq_words, Wq_scales, 0, STAGE_BANKS)
-        tables = build_rotation_tables(nc, keep)
-        load_stage(Wq_words, Wq_scales, STAGE_COLS, 1)
-        load_stage(Wk_words, Wk_scales, 0, 1)
-        load_stage(Wk_words, Wk_scales, STAGE_COLS, 1)
+        for words_in, scales_in in ((Wq_words, Wq_scales), (Wk_words, Wk_scales)):
+            for col0 in range(0, HEADS * HEAD, STAGE_COLS):
+                n = len(stages)
+                plane = keep.tile([P, PASSES, STAGE_COLS], U8, name="plane%d" % n, align_bytes=64)
+                nc.vector.memset(plane[:].bitcast(I32), 0)
+                load_scale_rows(nc, plane, scales_in, col0)
+                words = keep.tile([P, PASSES, 2 * STAGE_COLS], U8, name="words%d" % n, align_bytes=64)
+                for g in range(PASSES):
+                    nc.sync.dma_start(
+                        out=words[:, g, :].bitcast(I32),
+                        in_=words_in[g, :, 2 * col0 : 2 * (col0 + STAGE_COLS)].bitcast(I32),
+                    )
+                stages.append((plane, words))
 
         ident = keep.tile([P, P], F32)
         make_identity(nc, ident[:])
@@ -160,29 +153,35 @@ def tile_mla_pa_kernel(tc, x, Wq_words, Wq_scales, Wk_words, Wk_scales, out_0, o
                 in_=grouped[:, b].rearrange("p g m t -> p (g m t)"),
             )
 
+        tables = build_rotation_tables(nc, keep)
+
         for n, (plane, words) in enumerate(stages):
-            out, half = (out_0, out_1)[n // STAGES], n % STAGES
+            out, col0 = (out_0, out_1)[n // STAGES], (n % STAGES) * STAGE_COLS
             for b in range(SEQS):
+                banks = range(STAGE_BANKS)
+                if b == 0:
+                    order = [(g, j) for g in range(PASSES) for j in banks]
+                else:
+                    order = [(g, j) for j in banks for g in range(PASSES)]
+                accs = [psum.tile([P, BANK], F32, name="acc%d" % j, tag="bank") for j in banks]
+                for g, j in order:
+                    nc.tensor.matmul_mx(
+                        out=accs[j][:],
+                        lhsT=x_codes[:, b, g, :].bitcast(FP8X4),
+                        lhsT_scale=x_scales[:, b, g, :],
+                        rhs=words[:, g, 2 * j * BANK : 2 * (j + 1) * BANK].bitcast(FP4X4),
+                        rhs_scale=plane[:, g, j * BANK : (j + 1) * BANK],
+                        start=(g == 0),
+                        stop=(g == PASSES - 1),
+                    )
+
                 result = keep.tile([P, STAGE_HEADS, HEAD], F32, name="result%d_%d" % (n, b))
                 flat = result[:].rearrange("p h d -> p (h d)")
-                out_flat = out[b].rearrange("s h d -> s (h d)")[
-                    :, half * STAGE_COLS : (half + 1) * STAGE_COLS
-                ]
+                out_flat = out[b].rearrange("s h d -> s (h d)")[:, col0 : col0 + STAGE_COLS]
                 last = n == len(stages) - 1 and b == SEQS - 1
-                for j in range(STAGE_BANKS):
+                for j in banks:
                     bank_cols = slice(j * BANK, (j + 1) * BANK)
-                    acc = psum.tile([P, BANK], F32, tag="bank")
-                    for g in range(PASSES):
-                        nc.tensor.matmul_mx(
-                            out=acc[:],
-                            lhsT=x_codes[:, b, g, :].bitcast(FP8X4),
-                            lhsT_scale=x_scales[:, b, g, :],
-                            rhs=words[:, g, 2 * j * BANK : 2 * (j + 1) * BANK].bitcast(FP4X4),
-                            rhs_scale=plane[:, g, bank_cols],
-                            start=(g == 0),
-                            stop=(g == PASSES - 1),
-                        )
-                    nc.scalar.copy(out=flat[:, bank_cols], in_=acc[:])
+                    nc.scalar.copy(out=flat[:, bank_cols], in_=accs[j][:])
                     mine = [h for h in range(STAGE_HEADS) if (h * HEAD + NOPE) // BANK == j]
                     rotate(nc, work, result[:, mine[0] : mine[-1] + 1, NOPE:HEAD], tables)
                     if last:

@@ -35,6 +35,9 @@ STAGES = HEADS // STAGE_HEADS
 SCALE_ROWS = K_PASS // 32
 ROUND = 1.5 * 2.0**23
 
+WARM_FIRST = 5
+WARM_SECOND = 4
+
 FLOPS = 2 * SEQS * P * DIM * 2 * HEADS * HEAD
 
 
@@ -108,6 +111,16 @@ def tile_mla_pa_kernel(tc, x, Wq_words, Wq_scales, Wk_words, Wk_scales, out_0, o
         nc.vector.memset(zero[:], 0.0)
         nc.scalar.activation(out=zero[:], in_=zero[:], func=ACT.Sin)
 
+        zeros = keep.tile([P, BANK], BF16)
+        nc.gpsimd.memset(zeros[:], 0.0)
+        idle = psum.tile([P, BANK], F32, tag="bank")
+
+        def warm(count):
+            for i in range(count):
+                nc.tensor.matmul(idle[:], lhsT=zeros[:, 0:P], rhs=zeros[:], start=True, stop=True)
+
+        warm(WARM_FIRST)
+
         x_sb = keep.tile([P, SEQS, DIM], BF16)
         for b in range(SEQS):
             nc.sync.dma_start(out=x_sb[:, b, :], in_=x[b])
@@ -153,13 +166,15 @@ def tile_mla_pa_kernel(tc, x, Wq_words, Wq_scales, Wk_words, Wk_scales, out_0, o
                 in_=grouped[:, b].rearrange("p g m t -> p (g m t)"),
             )
 
+        warm(WARM_SECOND)
+
         tables = build_rotation_tables(nc, keep)
 
         for n, (plane, words) in enumerate(stages):
             out, col0 = (out_0, out_1)[n // STAGES], (n % STAGES) * STAGE_COLS
             for b in range(SEQS):
                 banks = range(STAGE_BANKS)
-                if b == 0:
+                if b == 0 and n < len(stages) - 1:
                     order = [(g, j) for g in range(PASSES) for j in banks]
                 else:
                     order = [(g, j) for j in banks for g in range(PASSES)]

@@ -28,6 +28,7 @@ PACK = 4
 K_PASS = P * PACK
 PASSES = DIM // K_PASS
 BANK = 512
+QUARTER = BANK // 4
 STAGE_HEADS = 8
 STAGE_COLS = STAGE_HEADS * HEAD
 STAGE_BANKS = STAGE_COLS // BANK
@@ -68,35 +69,28 @@ def build_rotation_tables(nc, keep):
     nc.vector.tensor_sub(turns[:], turns[:], whole[:])
 
     cos_twice = keep.tile([P, PAIRS, 2], F32)
-    sin_minus = keep.tile([P, PAIRS], F32)
-    sin_plus = keep.tile([P, PAIRS], F32)
+    sin_signed = keep.tile([P, PAIRS, 2], F32)
     nc.scalar.activation(
         out=cos_twice[:], in_=turns[:, 0, :].unsqueeze(2).to_broadcast([P, PAIRS, 2]),
         func=ACT.Sin, scale=2.0 * math.pi,
     )
-    nc.scalar.activation(out=sin_minus[:], in_=turns[:, 1, :], func=ACT.Sin, scale=-2.0 * math.pi)
-    nc.scalar.activation(out=sin_plus[:], in_=turns[:, 1, :], func=ACT.Sin, scale=2.0 * math.pi)
-    return cos_twice, sin_minus, sin_plus
+    for side, sign in enumerate((-1.0, 1.0)):
+        nc.scalar.activation(
+            out=sin_signed[:, :, side], in_=turns[:, 1, :], func=ACT.Sin, scale=sign * 2.0 * math.pi
+        )
+    return cos_twice, sin_signed
 
 
 def rotate(nc, work, rope, tables):
-    cos_twice, sin_minus, sin_plus = tables
+    cos_twice, sin_signed = tables
     heads = rope.shape[1]
     pairs = rope.rearrange("p h (i two) -> p h i two", two=2)
-    straight = work.tile([P, heads, PAIRS, 2], F32, tag="straight")
-    nc.vector.tensor_mul(
-        straight[:], pairs, cos_twice[:].unsqueeze(1).to_broadcast([P, heads, PAIRS, 2])
-    )
-    crossed = work.tile([P, heads, 2, PAIRS], F32, tag="crossed")
-    nc.vector.tensor_mul(
-        crossed[:, :, 0, :], pairs[:, :, :, 1],
-        sin_minus[:].unsqueeze(1).to_broadcast([P, heads, PAIRS]),
-    )
-    nc.vector.tensor_mul(
-        crossed[:, :, 1, :], pairs[:, :, :, 0],
-        sin_plus[:].unsqueeze(1).to_broadcast([P, heads, PAIRS]),
-    )
-    nc.vector.tensor_add(pairs, straight[:], crossed[:].rearrange("p h two i -> p h i two"))
+    whole = [P, heads, PAIRS, 2]
+    crossed = work.tile(whole, F32, tag="crossed")
+    nc.vector.tensor_mul(crossed[:], pairs[:, :, :, ::-1], sin_signed[:].unsqueeze(1).to_broadcast(whole))
+    straight = work.tile(whole, F32, tag="straight")
+    nc.vector.tensor_mul(straight[:], pairs, cos_twice[:].unsqueeze(1).to_broadcast(whole))
+    nc.vector.tensor_add(pairs, straight[:], crossed[:])
 
 
 def tile_mla_pa_kernel(tc, x, Wq_words, Wq_scales, Wk_words, Wk_scales, out_0, out_1):
@@ -170,36 +164,55 @@ def tile_mla_pa_kernel(tc, x, Wq_words, Wq_scales, Wk_words, Wk_scales, out_0, o
 
         tables = build_rotation_tables(nc, keep)
 
-        for n, (plane, words) in enumerate(stages):
+        def multiply(acc, n, b, g, first, width):
+            plane, words = stages[n]
+            nc.tensor.matmul_mx(
+                out=acc,
+                lhsT=x_codes[:, b, g, :].bitcast(FP8X4),
+                lhsT_scale=x_scales[:, b, g, :],
+                rhs=words[:, g, 2 * first : 2 * (first + width)].bitcast(FP4X4),
+                rhs_scale=plane[:, g, first : first + width],
+                start=(g == 0),
+                stop=(g == PASSES - 1),
+            )
+
+        for n in range(len(stages)):
             out, col0 = (out_0, out_1)[n // STAGES], (n % STAGES) * STAGE_COLS
             for b in range(SEQS):
-                banks = range(STAGE_BANKS)
-                if b == 0 and n < len(stages) - 1:
-                    order = [(g, j) for g in range(PASSES) for j in banks]
-                else:
-                    order = [(g, j) for j in banks for g in range(PASSES)]
-                accs = [psum.tile([P, BANK], F32, name="acc%d" % j, tag="bank") for j in banks]
-                for g, j in order:
-                    nc.tensor.matmul_mx(
-                        out=accs[j][:],
-                        lhsT=x_codes[:, b, g, :].bitcast(FP8X4),
-                        lhsT_scale=x_scales[:, b, g, :],
-                        rhs=words[:, g, 2 * j * BANK : 2 * (j + 1) * BANK].bitcast(FP4X4),
-                        rhs_scale=plane[:, g, j * BANK : (j + 1) * BANK],
-                        start=(g == 0),
-                        stop=(g == PASSES - 1),
-                    )
-
                 result = keep.tile([P, STAGE_HEADS, HEAD], F32, name="result%d_%d" % (n, b))
                 flat = result[:].rearrange("p h d -> p (h d)")
                 out_flat = out[b].rearrange("s h d -> s (h d)")[:, col0 : col0 + STAGE_COLS]
                 last = n == len(stages) - 1 and b == SEQS - 1
-                for j in banks:
-                    bank_cols = slice(j * BANK, (j + 1) * BANK)
-                    nc.scalar.copy(out=flat[:, bank_cols], in_=accs[j][:])
-                    mine = [h for h in range(STAGE_HEADS) if (h * HEAD + NOPE) // BANK == j]
-                    rotate(nc, work, result[:, mine[0] : mine[-1] + 1, NOPE:HEAD], tables)
-                    if last:
-                        nc.sync.dma_start(out=out_flat[:, bank_cols], in_=flat[:, bank_cols])
                 if not last:
-                    nc.sync.dma_start(out=out_flat, in_=flat)
+                    pieces = [
+                        (0, BANK, (0, 2), None),
+                        (BANK, BANK, (2, 5), None),
+                        (2 * BANK, BANK, (5, 8), (0, STAGE_COLS)),
+                    ]
+                else:
+                    pieces = [
+                        (2 * BANK, BANK, (5, 8), (2 * BANK, 3 * BANK)),
+                        (BANK, BANK, (2, 5), (BANK, 2 * BANK)),
+                        (QUARTER, QUARTER, None, None),
+                        (2 * QUARTER, QUARTER, (0, 2), (QUARTER, 3 * QUARTER)),
+                        (0, QUARTER, None, (0, QUARTER)),
+                        (3 * QUARTER, QUARTER, None, (3 * QUARTER, BANK)),
+                    ]
+                accs = [
+                    psum.tile([P, width], F32, name="acc%d" % i, tag="bank")
+                    for i, (first, width, heads, store) in enumerate(pieces)
+                ]
+                if b == 0 and n < len(stages) - 1:
+                    order = [(g, i) for g in range(PASSES) for i in range(len(pieces))]
+                else:
+                    order = [(g, i) for i in range(len(pieces)) for g in range(PASSES)]
+                for g, i in order:
+                    multiply(accs[i][:], n, b, g, pieces[i][0], pieces[i][1])
+                for acc, (first, width, heads, store) in zip(accs, pieces):
+                    nc.scalar.copy(out=flat[:, first : first + width], in_=acc[:])
+                    if heads is not None:
+                        rotate(nc, work, result[:, heads[0] : heads[1], NOPE:HEAD], tables)
+                    if store is not None:
+                        nc.sync.dma_start(
+                            out=out_flat[:, store[0] : store[1]], in_=flat[:, store[0] : store[1]]
+                        )

@@ -204,6 +204,10 @@ def tile_mla_pa_kernel(tc, x, Wq_words, Wq_scales, Wk_words, Wk_scales, out_0, o
                 ]
                 if b == 0 and n < len(stages) - 1:
                     order = [(g, i) for g in range(PASSES) for i in range(len(pieces))]
+                elif b == 0:
+                    half = PASSES // 2
+                    order = [(g, i) for g in range(half) for i in range(len(pieces))]
+                    order += [(g, i) for i in range(len(pieces)) for g in range(half, PASSES)]
                 else:
                     order = [(g, i) for i in range(len(pieces)) for g in range(PASSES)]
                 for g, i in order:

import math
from contextlib import ExitStack

import concourse.mybir as mybir
from concourse.masks import make_identity

F32 = mybir.dt.float32
BF16 = mybir.dt.bfloat16
I32 = mybir.dt.int32
U32 = mybir.dt.uint32
U8 = mybir.dt.uint8
FP8X4 = mybir.dt.float8_e4m3fn_x4
FP4X4 = mybir.dt.float4_e2m1fn_x4
ALU = mybir.AluOpType
ACT = mybir.ActivationFunctionType

P = 128
SEQS = 2
DIM = 2048
HEADS = 16
NOPE = 128
ROPE = 64
HEAD = NOPE + ROPE
PAIRS = ROPE // 2
BASE = 10000.0

PACK = 4
K_PASS = P * PACK
PASSES = DIM // K_PASS
BANK = 512
QUARTER = BANK // 4
STAGE_HEADS = 8
STAGE_COLS = STAGE_HEADS * HEAD
STAGE_BANKS = STAGE_COLS // BANK
STAGES = HEADS // STAGE_HEADS
SCALE_ROWS = K_PASS // 32
ROUND = 1.5 * 2.0**23

WARM_FIRST = 5
WARM_SECOND = 4

FLOPS = 2 * SEQS * P * DIM * 2 * HEADS * HEAD


def load_scale_rows(nc, plane, scales, col0):
    by_row = scales.rearrange("g q n -> q g n")
    for q in range(SCALE_ROWS // 2):
        first = 32 * (q // 4) + q % 4
        nc.sync.dma_start(
            out=plane[first:P:64, :, :].bitcast(I32),
            in_=by_row[q : SCALE_ROWS : SCALE_ROWS // 2, :, col0 : col0 + STAGE_COLS].bitcast(I32),
        )


def build_rotation_tables(nc, keep):
    position = keep.tile([P, 1], I32)
    nc.gpsimd.iota(position[:], pattern=[[0, 1]], base=0, channel_multiplier=1)
    turns = keep.tile([P, 2, PAIRS], F32)
    nc.vector.tensor_scalar_mul(turns[:, 1, 0:1], position[:], 0.5 / math.pi)
    for width in (1, 2, 4, 8, 16):
        nc.vector.tensor_scalar_mul(
            turns[:, 1, width : 2 * width], turns[:, 1, 0:width], BASE ** (-2.0 * width / ROPE)
        )
    nc.vector.tensor_scalar_add(turns[:, 0, :], turns[:, 1, :], 0.25)
    whole = keep.tile([P, 2, PAIRS], F32)
    nc.vector.tensor_scalar(
        out=whole[:], in0=turns[:], scalar1=ROUND, scalar2=ROUND, op0=ALU.add, op1=ALU.subtract
    )
    nc.vector.tensor_sub(turns[:], turns[:], whole[:])

    cos_twice = keep.tile([P, PAIRS, 2], F32)
    sin_signed = keep.tile([P, PAIRS, 2], F32)
    nc.scalar.activation(
        out=cos_twice[:], in_=turns[:, 0, :].unsqueeze(2).to_broadcast([P, PAIRS, 2]),
        func=ACT.Sin, scale=2.0 * math.pi,
    )
    for side, sign in enumerate((-1.0, 1.0)):
        nc.scalar.activation(
            out=sin_signed[:, :, side], in_=turns[:, 1, :], func=ACT.Sin, scale=sign * 2.0 * math.pi
        )
    return cos_twice, sin_signed


def rotate(nc, work, rope, tables):
    cos_twice, sin_signed = tables
    heads = rope.shape[1]
    pairs = rope.rearrange("p h (i two) -> p h i two", two=2)
    whole = [P, heads, PAIRS, 2]
    crossed = work.tile(whole, F32, tag="crossed")
    nc.vector.tensor_mul(crossed[:], pairs[:, :, :, ::-1], sin_signed[:].unsqueeze(1).to_broadcast(whole))
    straight = work.tile(whole, F32, tag="straight")
    nc.vector.tensor_mul(straight[:], pairs, cos_twice[:].unsqueeze(1).to_broadcast(whole))
    nc.vector.tensor_add(pairs, straight[:], crossed[:])


def tile_mla_pa_kernel(tc, x, Wq_words, Wq_scales, Wk_words, Wk_scales, out_0, out_1):
    nc = tc.nc
    with ExitStack() as ctx:
        keep = ctx.enter_context(tc.tile_pool(name="keep", bufs=1))
        work = ctx.enter_context(tc.tile_pool(name="work", bufs=3))
        psum = ctx.enter_context(tc.psum_pool(name="psum", bufs=8))
        ctx.enter_context(tc.manual_schedule())

        zero = keep.tile([P, 1], F32)
        nc.vector.memset(zero[:], 0.0)
        nc.scalar.activation(out=zero[:], in_=zero[:], func=ACT.Sin)

        zeros = keep.tile([P, BANK], BF16)
        nc.gpsimd.memset(zeros[:], 0.0)
        idle = psum.tile([P, BANK], F32, tag="bank")

        def warm(count):
            for i in range(count):
                nc.tensor.matmul(idle[:], lhsT=zeros[:, 0:P], rhs=zeros[:], start=True, stop=True)

        warm(WARM_FIRST)

        x_sb = keep.tile([P, SEQS, DIM], BF16)
        for b in range(SEQS):
            nc.sync.dma_start(out=x_sb[:, b, :], in_=x[b])

        stages = []
        for words_in, scales_in in ((Wq_words, Wq_scales), (Wk_words, Wk_scales)):
            for col0 in range(0, HEADS * HEAD, STAGE_COLS):
                n = len(stages)
                plane = keep.tile([P, PASSES, STAGE_COLS], U8, name="plane%d" % n, align_bytes=64)
                nc.vector.memset(plane[:].bitcast(I32), 0)
                load_scale_rows(nc, plane, scales_in, col0)
                words = keep.tile([P, PASSES, 2 * STAGE_COLS], U8, name="words%d" % n, align_bytes=64)
                for g in range(PASSES):
                    nc.sync.dma_start(
                        out=words[:, g, :].bitcast(I32),
                        in_=words_in[g, :, 2 * col0 : 2 * (col0 + STAGE_COLS)].bitcast(I32),
                    )
                stages.append((plane, words))

        ident = keep.tile([P, P], F32)
        make_identity(nc, ident[:])
        grouped = keep.tile([P, SEQS, PASSES, P, PACK], BF16, align_bytes=64)
        x_codes = keep.tile([P, SEQS, PASSES, P], U32, align_bytes=64)
        x_scales = keep.tile([P, SEQS, PASSES, P], U8, align_bytes=64)
        for b in range(SEQS):
            x_words = x_sb[:, b, :].bitcast(F32)
            for pair in range(PASSES // 2):
                bank = psum.tile([P, BANK], F32, tag="bank")
                for slot in range(4):
                    g, u = 2 * pair + slot // 2, slot % 2
                    nc.tensor.transpose(
                        bank[:, slot * P : (slot + 1) * P],
                        x_words[:, 256 * g + u : 256 * (g + 1) : 2],
                        ident[:],
                    )
                nc.scalar.copy(
                    out=grouped[:, b, 2 * pair : 2 * pair + 2, :, :].bitcast(F32),
                    in_=bank[:].rearrange("p (g u m) -> p g m u", g=2, u=2),
                )
            nc.vector.quantize_mx(
                out=x_codes[:, b].rearrange("p g m -> p (g m)").bitcast(FP8X4),
                scales=x_scales[:, b].rearrange("p g m -> p (g m)"),
                in_=grouped[:, b].rearrange("p g m t -> p (g m t)"),
            )

        warm(WARM_SECOND)

        tables = build_rotation_tables(nc, keep)

        def multiply(acc, n, b, g, first, width):
            plane, words = stages[n]
            nc.tensor.matmul_mx(
                out=acc,
                lhsT=x_codes[:, b, g, :].bitcast(FP8X4),
                lhsT_scale=x_scales[:, b, g, :],
                rhs=words[:, g, 2 * first : 2 * (first + width)].bitcast(FP4X4),
                rhs_scale=plane[:, g, first : first + width],
                start=(g == 0),
                stop=(g == PASSES - 1),
            )

        for n in range(len(stages)):
            out, col0 = (out_0, out_1)[n // STAGES], (n % STAGES) * STAGE_COLS
            for b in range(SEQS):
                result = keep.tile([P, STAGE_HEADS, HEAD], F32, name="result%d_%d" % (n, b))
                flat = result[:].rearrange("p h d -> p (h d)")
                out_flat = out[b].rearrange("s h d -> s (h d)")[:, col0 : col0 + STAGE_COLS]
                last = n == len(stages) - 1 and b == SEQS - 1
                if not last:
                    pieces = [
                        (0, BANK, (0, 2), None),
                        (BANK, BANK, (2, 5), None),
                        (2 * BANK, BANK, (5, 8), (0, STAGE_COLS)),
                    ]
                else:
                    pieces = [
                        (2 * BANK, BANK, (5, 8), (2 * BANK, 3 * BANK)),
                        (BANK, BANK, (2, 5), (BANK, 2 * BANK)),
                        (QUARTER, QUARTER, None, None),
                        (2 * QUARTER, QUARTER, (0, 2), (QUARTER, 3 * QUARTER)),
                        (0, QUARTER, None, (0, QUARTER)),
                        (3 * QUARTER, QUARTER, None, (3 * QUARTER, BANK)),
                    ]
                accs = [
                    psum.tile([P, width], F32, name="acc%d" % i, tag="bank")
                    for i, (first, width, heads, store) in enumerate(pieces)
                ]
                if b == 0 and n < len(stages) - 1:
                    order = [(g, i) for g in range(PASSES) for i in range(len(pieces))]
                elif b == 0:
                    half = PASSES // 2
                    order = [(g, i) for g in range(half) for i in range(len(pieces))]
                    order += [(g, i) for i in range(len(pieces)) for g in range(half, PASSES)]
                else:
                    order = [(g, i) for i in range(len(pieces)) for g in range(PASSES)]
                for g, i in order:
                    multiply(accs[i][:], n, b, g, pieces[i][0], pieces[i][1])
                for acc, (first, width, heads, store) in zip(accs, pieces):
                    nc.scalar.copy(out=flat[:, first : first + width], in_=acc[:])
                    if heads is not None:
                        rotate(nc, work, result[:, heads[0] : heads[1], NOPE:HEAD], tables)
                    if store is not None:
                        nc.sync.dma_start(
                            out=out_flat[:, store[0] : store[1]], in_=flat[:, store[0] : store[1]]
                        )
